import numpy as np
import ml_dtypes


def mxq(x, axis, fmt="e4m3"):
    dtype, down = {"e4m3": (ml_dtypes.float8_e4m3fn, 7), "e5m2": (ml_dtypes.float8_e5m2, 14)}[fmt]
    v = np.moveaxis(np.asarray(x, np.float32).astype(ml_dtypes.bfloat16).astype(np.float64), axis, -1)
    blocks = v.reshape(v.shape[:-1] + (-1, 32))
    amax = np.abs(blocks).max(-1, keepdims=True)
    byte = np.maximum(np.where(amax > 0, np.frexp(amax)[1] - 1 + 127, 0) - down, 1)
    scale = np.exp2(byte - 127.0)
    codes = (blocks / scale).astype(np.float32).astype(dtype).astype(np.float64)
    return np.moveaxis((codes * scale).reshape(v.shape), -1, axis)


WIDE = False


def mx_kscale(k):
    if not WIDE:
        return np.ones(k)
    levels = np.array([30, -30])
    if k % 512:
        return np.exp2(np.random.permutation(np.resize(levels, k // 32))).repeat(32)
    a = np.empty((k // 512, 16))
    for p in range(k // 512):
        a[p, :8] = np.random.permutation(np.resize(levels, 8))
        for g in range(8):
            far = levels[np.abs(levels - a[p, g]) >= 10]
            a[p, g + 8] = far[np.random.randint(len(far))]
    return np.exp2(a.ravel()).repeat(32)


BF16 = ml_dtypes.bfloat16


def bf(x):
    return np.asarray(x, np.float32).astype(BF16)


def f64(x):
    return np.asarray(x).astype(np.float64)


E2M1 = np.array([0.0, 0.5, 1.0, 1.5, 2.0, 3.0, 4.0, 6.0, -0.0, -0.5, -1.0, -1.5, -2.0, -3.0, -4.0, -6.0])


def pack_weight(w, fmt):
    k, n = w.shape
    w = f64(bf(w)).reshape(k // 32, 32, n)
    amax = np.abs(w).max(1)
    if fmt == "e4m3":
        byte = np.frexp(amax)[1] - 1 + 127 - 7
    else:
        mant, ex = np.frexp(amax / 6.0)
        byte = np.where(mant > 0.5, ex, ex - 1) + 127
    byte = np.clip(np.where(amax > 0, byte, 1), 1, 254)
    scaled = (w * np.exp2(127.0 - byte)[:, None, :]).reshape(k, n).astype(np.float32)
    by_word = np.ascontiguousarray(scaled.reshape(k // 512, 128, 4, n).transpose(0, 1, 3, 2))
    if fmt == "e4m3":
        words = by_word.astype(ml_dtypes.float8_e4m3fn).view(np.uint8)
    else:
        c = by_word.astype(ml_dtypes.float4_e2m1fn).view(np.uint8) & 0xF
        words = c[..., 0::2] | (c[..., 1::2] << 4)
    return np.ascontiguousarray(words), np.ascontiguousarray(byte.astype(np.uint8).reshape(k // 512, 16, n))


def unpack_weight(words, scales, fmt):
    g, p, n, _ = words.shape
    if fmt == "e4m3":
        vals = np.ascontiguousarray(words).view(ml_dtypes.float8_e4m3fn).astype(np.float64)
    else:
        nib = np.empty((g, p, n, 4), np.uint8)
        nib[..., 0::2] = words & 0xF
        nib[..., 1::2] = words >> 4
        vals = E2M1[nib]
    vals = vals * np.repeat(np.exp2(scales.astype(np.float64) - 127.0), 8, axis=1)[..., None]
    return vals.transpose(0, 1, 3, 2).reshape(g * 512, n)

def pack4(w):
    words, scales = pack_weight(w, "e2m1")
    return words.reshape(words.shape[0], 128, -1), scales


def unpack4(words, scales):
    return unpack_weight(words.reshape(words.shape[0], 128, -1, 2), scales, "e2m1")


B, S, C, H, D = 4, 512, 1024, 8, 128
E = H * D


def rope_tables():
    inv_freq = 1.0 / (10000.0 ** (np.arange(0, D, 2) / D))
    emb = np.repeat(np.outer(np.arange(S), inv_freq), 2, axis=1)
    return np.cos(emb), np.sin(emb)


def rope(t, cos, sin):
    tr = t[..., 0::2]
    ti = t[..., 1::2]
    t_rot = np.stack([-ti, tr], axis=-1).reshape(t.shape)
    return t * cos + t_rot * sin


def setup_inputs():
    s = mx_kscale(C)
    cos, sin = rope_tables()
    x = bf(np.random.standard_normal((B, S, C)) * s)
    Wq = np.random.standard_normal((E, C)) / np.sqrt(C) / s[None, :]
    Wq_words, Wq_scales = pack4(np.ascontiguousarray(Wq.T))
    bq = bf(np.random.standard_normal(E) * 0.1)
    return {"x": x,
            "cos": bf(cos), "sin": bf(sin),
            "Wq_words": Wq_words, "Wq_scales": Wq_scales,
            "bq": bq}


def reference(x, cos, sin, Wq_words, Wq_scales, bq):
    y = (mxq(f64(x), 2, "e5m2") @ unpack4(Wq_words, Wq_scales)) + f64(bq)
    q = y.reshape(B, S, H, D).transpose(0, 2, 1, 3)
    return np.maximum(rope(q, f64(cos), f64(sin)), 0.0)

@@ -1,0 +1,208 @@
+from contextlib import ExitStack
+
+import concourse.mybir as mybir
+from concourse.masks import make_identity
+
+B, S, C, H, D = 4, 512, 1024, 8, 128
+FLOPS = 2 * B * S * C * H * D
+
+F32 = mybir.dt.float32
+BF16 = mybir.dt.bfloat16
+U32 = mybir.dt.uint32
+U8 = mybir.dt.uint8
+I32 = mybir.dt.int32
+E5X4 = mybir.dt.float8_e5m2_x4
+E2X4 = mybir.dt.float4_e2m1fn_x4
+ADD = mybir.AluOpType.add
+MULT = mybir.AluOpType.mult
+RELU = mybir.ActivationFunctionType.Relu
+
+P = 128
+G = 2
+A = 4
+J = 4
+UNITS = B * J
+LAG = 3
+LEAD = 5
+
+
+def tile_lineartransformerblock_pa_kernel(tc, x, cos, sin, Wq_words, Wq_scales, bq, out):
+    nc = tc.nc
+    with ExitStack() as ctx:
+        const = ctx.enter_context(tc.tile_pool(name="const", bufs=1))
+        work = ctx.enter_context(tc.tile_pool(name="work", bufs=2))
+        psum = ctx.enter_context(tc.psum_pool(name="psum", bufs=2))
+        ctx.enter_context(tc.manual_schedule())
+
+        cos_raw = const.tile([P, A, D], BF16, name="cos_raw", tag="cos_raw")
+        sin_raw = const.tile([P, A, D], BF16, name="sin_raw", tag="sin_raw")
+        nc.sync.dma_start(out=cos_raw[:], in_=cos.rearrange("(p a) d -> p a d", a=A))
+        nc.sync.dma_start(out=sin_raw[:], in_=sin.rearrange("(p a) d -> p a d", a=A))
+
+        w_raw = const.tile([P, G, 2 * H * D], U8, name="w_raw", tag="w_raw", align_bytes=64)
+        for g in range(G):
+            nc.sync.dma_start(out=w_raw[:, g, :].bitcast(I32), in_=Wq_words[g].bitcast(I32))
+
+        ws_raw = const.tile([P, G, H * D], U8, name="ws_raw", tag="ws_raw", align_bytes=64)
+        nc.vector.memset(ws_raw[:].rearrange("p g n -> p (g n)").bitcast(I32), 0)
+        for q4 in range(4):
+            nc.sync.dma_start(
+                out=ws_raw[32 * q4 : 32 * q4 + 4, :, :].bitcast(I32),
+                in_=Wq_scales[:, 4 * q4 : 4 * q4 + 4, :].rearrange("g r n -> r g n").bitcast(I32),
+            )
+
+        x_sb = []
+        for b in range(B):
+            x_sb.append(const.tile([P, A, C], BF16, name="x_sb%d" % b, tag="x_sb%d" % b))
+        x_view = x.rearrange("b (p a) k -> b p a k", a=A)
+        for a in range(A):
+            nc.sync.dma_start(out=x_sb[0][:, a, :], in_=x_view[0, :, a, :])
+        bias_bf = const.tile([P, J, 2], BF16, name="bias_bf", tag="bias_bf")
+        nc.sync.dma_start(out=bias_bf[:], in_=bq.rearrange("(j q r) -> q j r", j=J, r=2))
+        for b in range(1, B):
+            nc.sync.dma_start(out=x_sb[b][:], in_=x_view[b])
+
+        ident_f = const.tile([P, P], F32, name="ident_f", tag="ident_f")
+        make_identity(nc, ident_f[:])
+        ident_b = const.tile([P, P], BF16, name="ident_b", tag="ident_b")
+        make_identity(nc, ident_b[:])
+
+        warm_in = const.tile([P, 1], F32, name="warm_in", tag="warm_in")
+        warm_out = const.tile([P, 1], F32, name="warm_out", tag="warm_out")
+        nc.vector.memset(warm_in[:], 0.0)
+        nc.scalar.activation(out=warm_out[:], in_=warm_in[:], func=RELU)
+
+        stg = const.tile([P, 4, A, P], BF16, name="stg", tag="stg")
+        specs = ((cos_raw, 0, 1.0), (sin_raw, 0, -1.0), (cos_raw, 1, 1.0), (sin_raw, 1, 1.0))
+        for t in range(4):
+            src, par, sign = specs[t]
+            for hh in range(2):
+                nc.vector.tensor_scalar_mul(
+                    out=stg[:, t, :, 64 * hh : 64 * (hh + 1)], in0=src[:, :, par::2], scalar1=sign
+                )
+
+        wp = const.tile([P, G, J, 2, 2 * P], U8, name="wp", tag="wp", align_bytes=64)
+        wsp = const.tile([P, G, J, 2, P], U8, name="wsp", tag="wsp", align_bytes=64)
+        for g in range(G):
+            for par in range(2):
+                nc.vector.tensor_copy(
+                    out=wp[:, g, :, par, :].rearrange("p j (q t) -> p j q t", t=2),
+                    in_=w_raw[:, g, :].rearrange("p (j q r t) -> p j q r t", j=J, r=2, t=2)[:, :, :, par, :],
+                )
+                nc.vector.tensor_copy(
+                    out=wsp[:, g, :, par, :],
+                    in_=ws_raw[:, g, :].rearrange("p (j q r) -> p j q r", j=J, r=2)[:, :, :, par],
+                )
+        bias = const.tile([P, J, 2], F32, name="bias", tag="bias")
+        nc.vector.tensor_copy(out=bias[:], in_=bias_bf[:])
+
+        grouped = {}
+        xq = {}
+        xs = {}
+
+        def x_transpose(c):
+            b, a = c // A, c % A
+            if a == 0:
+                grouped[b] = work.tile([P, G, S, 2], F32, name="grouped", tag="grouped", align_bytes=64)
+            words = x_sb[b][:, a, :].bitcast(F32)
+            xt = psum.tile([P, G, 2, P], F32, name="xt", tag="xt")
+            for g in range(G):
+                for u in range(2):
+                    nc.tensor.transpose(xt[:, g, u, :], words[:, 256 * g + u : 256 * (g + 1) : 2], ident_f[:])
+            nc.scalar.copy(
+                out=grouped[b][:, :, P * a : P * (a + 1), :],
+                in_=xt[:].rearrange("p g u r -> p g r u"),
+            )
+
+        def quantize(b):
+            xq[b] = work.tile([P, G, S], U32, name="xq", tag="xq", align_bytes=64)
+            xs[b] = work.tile([P, G, S], U8, name="xs", tag="xs", align_bytes=64)
+            for g in range(G):
+                nc.vector.quantize_mx(
+                    out=xq[b][:, g, :].bitcast(E5X4),
+                    scales=xs[b][:, g, :],
+                    in_=grouped[b][:, g].rearrange("p c u -> p (c u)").bitcast(BF16),
+                )
+
+        acc = {}
+        prod = {}
+
+        def matmuls(n):
+            b, j = n // J, n % J
+            tiles = []
+            for par in range(2):
+                t = psum.tile([P, S], F32, name="acc%d" % par, tag="acc%d" % par)
+                for g in range(G):
+                    nc.tensor.matmul_mx(
+                        out=t[:],
+                        lhsT=wp[:, g, j, par, :].bitcast(E2X4),
+                        lhsT_scale=wsp[:, g, j, par, :],
+                        rhs=xq[b][:, g, :].bitcast(E5X4),
+                        rhs_scale=xs[b][:, g, :],
+                        start=(g == 0),
+                        stop=(g == G - 1),
+                    )
+                tiles.append(t)
+            acc[n] = tiles
+
+        def rope(n):
+            j = n % J
+            even, odd = acc[n]
+            ps = []
+            for k in range(4):
+                ps.append(work.tile([P, S], F32, name="p%d" % k, tag="p%d" % k, bufs=LAG + 1))
+            plan = ((even, 0, 0), (odd, 1, 1), (odd, 1, 2), (even, 0, 3))
+            for k in range(4):
+                a_t, par, t = plan[k]
+                nc.vector.scalar_tensor_tensor(
+                    out=ps[k][:], in0=a_t[:], scalar=bias[:, j, par : par + 1], in1=tabs[t][:], op0=ADD, op1=MULT
+                )
+                if k == 1:
+                    nc.gpsimd.tensor_tensor(out=ps[0][:], in0=ps[0][:], in1=ps[1][:], op=ADD)
+            nc.gpsimd.tensor_tensor(out=ps[2][:], in0=ps[2][:], in1=ps[3][:], op=ADD)
+            prod[n] = (ps[0], ps[2])
+
+        def finish(n):
+            b, j = n // J, n % J
+            ots = []
+            for half in range(2):
+                ots.append(psum.tile([P, 2, 2, P], F32, name="ot", tag="ot"))
+            for par in range(2):
+                for a in range(A):
+                    nc.tensor.transpose(ots[a // 2][:, a % 2, par, :], prod[n][par][:, P * a : P * (a + 1)], ident_f[:])
+            res = work.tile([P, 2, A, D], F32, name="res", tag="res", bufs=3)
+            for a in range(A):
+                nc.scalar.activation(
+                    out=res[:, :, a, :].rearrange("p h (i r) -> p h i r", r=2),
+                    in_=ots[a // 2][:, a % 2].rearrange("p r (h i) -> p h i r", h=2),
+                    func=RELU,
+                )
+            nc.sync.dma_start(
+                out=out[b, 2 * j : 2 * j + 2].rearrange("h (p a) d -> p h (a d)", a=A),
+                in_=res[:].rearrange("p h a d -> p h (a d)"),
+            )
+
+        for c in range(A):
+            x_transpose(c)
+        tabs = []
+        for t in range(4):
+            tp = psum.tile([P, S], BF16, name="tp", tag="ot")
+            for a in range(A):
+                nc.tensor.transpose(tp[:, P * a : P * (a + 1)], stg[:, t, a, :], ident_b[:])
+            tab = const.tile([P, S], BF16, name="tab%d" % t, tag="tab%d" % t)
+            nc.scalar.copy(out=tab[:], in_=tp[:])
+            tabs.append(tab)
+        quantize(0)
+        for c in range(A, LEAD):
+            x_transpose(c)
+
+        for n in range(UNITS + LAG):
+            if n + LEAD < UNITS:
+                x_transpose(n + LEAD)
+            if n >= LAG:
+                finish(n - LAG)
+            if n < UNITS:
+                matmuls(n)
+                if n % J == J - 1 and n + 1 < UNITS:
+                    quantize(n // J + 1)
+                rope(n)

@@ -16,6 +16,7 @@ E2X4 = mybir.dt.float4_e2m1fn_x4
 ADD = mybir.AluOpType.add
 MULT = mybir.AluOpType.mult
 RELU = mybir.ActivationFunctionType.Relu
+COPY = mybir.ActivationFunctionType.Copy
 
 P = 128
 G = 2
@@ -24,6 +25,8 @@ J = 4
 UNITS = B * J
 LAG = 3
 LEAD = 5
+PE_ADD = (2, 6, 10, 14, 15)
+WARM = (6, 2, 2)
 
 
 def tile_lineartransformerblock_pa_kernel(tc, x, cos, sin, Wq_words, Wq_scales, bq, out):
@@ -34,6 +37,17 @@ def tile_lineartransformerblock_pa_kernel(tc, x, cos, sin, Wq_words, Wq_scales, 
         psum = ctx.enter_context(tc.psum_pool(name="psum", bufs=2))
         ctx.enter_context(tc.manual_schedule())
 
+        bias_bf = const.tile([P, J, 2], BF16, name="bias_bf", tag="bias_bf")
+        nc.scalar.dma_start(out=bias_bf[:], in_=bq.rearrange("(j q r) -> q j r", j=J, r=2))
+
+        ws_raw = const.tile([P, G, H * D], U8, name="ws_raw", tag="ws_raw", align_bytes=64)
+        nc.gpsimd.memset(ws_raw[:].rearrange("p g n -> p (g n)").bitcast(F32), 0.0)
+        for q4 in range(4):
+            nc.sync.dma_start(
+                out=ws_raw[32 * q4 : 32 * q4 + 4, :, :].bitcast(I32),
+                in_=Wq_scales[:, 4 * q4 : 4 * q4 + 4, :].rearrange("g r n -> r g n").bitcast(I32),
+            )
+
         cos_raw = const.tile([P, A, D], BF16, name="cos_raw", tag="cos_raw")
         sin_raw = const.tile([P, A, D], BF16, name="sin_raw", tag="sin_raw")
         nc.sync.dma_start(out=cos_raw[:], in_=cos.rearrange("(p a) d -> p a d", a=A))
@@ -43,43 +57,56 @@ def tile_lineartransformerblock_pa_kernel(tc, x, cos, sin, Wq_words, Wq_scales, 
         for g in range(G):
             nc.sync.dma_start(out=w_raw[:, g, :].bitcast(I32), in_=Wq_words[g].bitcast(I32))
 
-        ws_raw = const.tile([P, G, H * D], U8, name="ws_raw", tag="ws_raw", align_bytes=64)
-        nc.vector.memset(ws_raw[:].rearrange("p g n -> p (g n)").bitcast(I32), 0)
-        for q4 in range(4):
-            nc.sync.dma_start(
-                out=ws_raw[32 * q4 : 32 * q4 + 4, :, :].bitcast(I32),
-                in_=Wq_scales[:, 4 * q4 : 4 * q4 + 4, :].rearrange("g r n -> r g n").bitcast(I32),
-            )
-
         x_sb = []
         for b in range(B):
             x_sb.append(const.tile([P, A, C], BF16, name="x_sb%d" % b, tag="x_sb%d" % b))
         x_view = x.rearrange("b (p a) k -> b p a k", a=A)
         for a in range(A):
             nc.sync.dma_start(out=x_sb[0][:, a, :], in_=x_view[0, :, a, :])
-        bias_bf = const.tile([P, J, 2], BF16, name="bias_bf", tag="bias_bf")
-        nc.sync.dma_start(out=bias_bf[:], in_=bq.rearrange("(j q r) -> q j r", j=J, r=2))
         for b in range(1, B):
             nc.sync.dma_start(out=x_sb[b][:], in_=x_view[b])
 
-        ident_f = const.tile([P, P], F32, name="ident_f", tag="ident_f")
-        make_identity(nc, ident_f[:])
-        ident_b = const.tile([P, P], BF16, name="ident_b", tag="ident_b")
-        make_identity(nc, ident_b[:])
-
+        zeros = const.tile([P, S], BF16, name="zeros", tag="zeros")
+        nc.vector.memset(zeros[:], 0.0)
         warm_in = const.tile([P, 1], F32, name="warm_in", tag="warm_in")
         warm_out = const.tile([P, 1], F32, name="warm_out", tag="warm_out")
         nc.vector.memset(warm_in[:], 0.0)
         nc.scalar.activation(out=warm_out[:], in_=warm_in[:], func=RELU)
 
-        stg = const.tile([P, 4, A, P], BF16, name="stg", tag="stg")
-        specs = ((cos_raw, 0, 1.0), (sin_raw, 0, -1.0), (cos_raw, 1, 1.0), (sin_raw, 1, 1.0))
-        for t in range(4):
-            src, par, sign = specs[t]
-            for hh in range(2):
-                nc.vector.tensor_scalar_mul(
-                    out=stg[:, t, :, 64 * hh : 64 * (hh + 1)], in0=src[:, :, par::2], scalar1=sign
-                )
+        ident_b = const.tile([P, P], BF16, name="ident_b", tag="ident_b")
+        make_identity(nc, ident_b[:])
+        ident_f = const.tile([P, P], F32, name="ident_f", tag="ident_f")
+        make_identity(nc, ident_f[:])
+
+        def dummy_matmuls(count):
+            for w in range(count):
+                d_ps = psum.tile([P, S], F32, name="d_ps", tag="acc0")
+                nc.tensor.matmul(out=d_ps[:], lhsT=zeros[:, 0:P], rhs=zeros[:], start=True, stop=True)
+
+        dummy_matmuls(WARM[0])
+
+        stg = const.tile([P, 2, 2, A, P], BF16, name="stg", tag="stg")
+
+        def spread(src, par):
+            return src[:, :, par::2].unsqueeze(2).to_broadcast([P, A, 2, D // 2])
+
+        def stg_view(e, t):
+            return stg[:, e, t].rearrange("p a (h i) -> p a h i", h=2)
+
+        nc.vector.tensor_copy(out=stg_view(0, 0), in_=spread(cos_raw, 0))
+        nc.vector.tensor_copy(out=stg_view(1, 1), in_=spread(cos_raw, 1))
+        nc.scalar.activation(out=stg_view(0, 1), in_=spread(sin_raw, 1), func=COPY)
+        nc.scalar.activation(out=stg_view(1, 0), in_=spread(sin_raw, 0), func=COPY, scale=-1.0)
+
+        tabs = []
+        for e in range(2):
+            tabs.append(const.tile([P, 2, S], BF16, name="tab%d" % e, tag="tab%d" % e))
+        for e, t, bank in ((0, 0, "ot"), (1, 1, "ot"), (0, 1, "acc1"), (1, 0, "acc1")):
+            tp = psum.tile([P, S], BF16, name="tp", tag=bank)
+            for a in range(A):
+                nc.tensor.transpose(tp[:, P * a : P * (a + 1)], stg[:, e, t, a, :], ident_b[:])
+            nc.scalar.copy(out=tabs[e][:, t, :], in_=tp[:])
+        dummy_matmuls(WARM[1])
 
         wp = const.tile([P, G, J, 2, 2 * P], U8, name="wp", tag="wp", align_bytes=64)
         wsp = const.tile([P, G, J, 2, P], U8, name="wsp", tag="wsp", align_bytes=64)
@@ -89,6 +116,8 @@ def tile_lineartransformerblock_pa_kernel(tc, x, cos, sin, Wq_words, Wq_scales, 
                     out=wp[:, g, :, par, :].rearrange("p j (q t) -> p j q t", t=2),
                     in_=w_raw[:, g, :].rearrange("p (j q r t) -> p j q r t", j=J, r=2, t=2)[:, :, :, par, :],
                 )
+        for g in range(G):
+            for par in range(2):
                 nc.vector.tensor_copy(
                     out=wsp[:, g, :, par, :],
                     in_=ws_raw[:, g, :].rearrange("p (j q r) -> p j q r", j=J, r=2)[:, :, :, par],
@@ -103,20 +132,32 @@ def tile_lineartransformerblock_pa_kernel(tc, x, cos, sin, Wq_words, Wq_scales, 
         def x_transpose(c):
             b, a = c // A, c % A
             if a == 0:
-                grouped[b] = work.tile([P, G, S, 2], F32, name="grouped", tag="grouped", align_bytes=64)
+                if b == 0:
+                    grouped[b] = const.tile([P, A, G, P, 2], F32, name="grouped0", tag="grouped0", align_bytes=64)
+                else:
+                    grouped[b] = work.tile([P, G, S, 2], F32, name="grouped", tag="grouped", align_bytes=64)
             words = x_sb[b][:, a, :].bitcast(F32)
             xt = psum.tile([P, G, 2, P], F32, name="xt", tag="xt")
             for g in range(G):
                 for u in range(2):
                     nc.tensor.transpose(xt[:, g, u, :], words[:, 256 * g + u : 256 * (g + 1) : 2], ident_f[:])
-            nc.scalar.copy(
-                out=grouped[b][:, :, P * a : P * (a + 1), :],
-                in_=xt[:].rearrange("p g u r -> p g r u"),
-            )
+            dst = grouped[b][:, a] if b == 0 else grouped[b][:, :, P * a : P * (a + 1), :]
+            nc.scalar.copy(out=dst, in_=xt[:].rearrange("p g u r -> p g r u"))
 
-        def quantize(b):
+        def new_codes(b):
             xq[b] = work.tile([P, G, S], U32, name="xq", tag="xq", align_bytes=64)
             xs[b] = work.tile([P, G, S], U8, name="xs", tag="xs", align_bytes=64)
+
+        def quantize_chunk(a):
+            for g in range(G):
+                nc.vector.quantize_mx(
+                    out=xq[0][:, g, P * a : P * (a + 1)].bitcast(E5X4),
+                    scales=xs[0][:, g, P * a : P * (a + 1)],
+                    in_=grouped[0][:, a, g].rearrange("p c u -> p (c u)").bitcast(BF16),
+                )
+
+        def quantize(b):
+            new_codes(b)
             for g in range(G):
                 nc.vector.quantize_mx(
                     out=xq[b][:, g, :].bitcast(E5X4),
@@ -147,62 +188,70 @@ def tile_lineartransformerblock_pa_kernel(tc, x, cos, sin, Wq_words, Wq_scales, 
 
         def rope(n):
             j = n % J
-            even, odd = acc[n]
-            ps = []
-            for k in range(4):
-                ps.append(work.tile([P, S], F32, name="p%d" % k, tag="p%d" % k, bufs=LAG + 1))
-            plan = ((even, 0, 0), (odd, 1, 1), (odd, 1, 2), (even, 0, 3))
-            for k in range(4):
-                a_t, par, t = plan[k]
-                nc.vector.scalar_tensor_tensor(
-                    out=ps[k][:], in0=a_t[:], scalar=bias[:, j, par : par + 1], in1=tabs[t][:], op0=ADD, op1=MULT
-                )
-                if k == 1:
+            pieces = 2 if n == UNITS - 1 else 1
+            width = S // pieces
+            prod[n] = []
+            for piece in range(pieces):
+                cols = slice(piece * width, (piece + 1) * width)
+                ps = []
+                for e in range(2):
+                    ps.append(work.tile([P, 2, width], F32, name="prod%d" % e, tag="prod%d" % e, bufs=LAG + 1))
+                    nc.vector.scalar_tensor_tensor(
+                        out=ps[e][:],
+                        in0=acc[n][e][:, cols].unsqueeze(1).to_broadcast([P, 2, width]),
+                        scalar=bias[:, j, e : e + 1],
+                        in1=tabs[e][:, :, cols],
+                        op0=ADD,
+                        op1=MULT,
+                    )
+                if n not in PE_ADD:
                     nc.gpsimd.tensor_tensor(out=ps[0][:], in0=ps[0][:], in1=ps[1][:], op=ADD)
-            nc.gpsimd.tensor_tensor(out=ps[2][:], in0=ps[2][:], in1=ps[3][:], op=ADD)
-            prod[n] = (ps[0], ps[2])
+                prod[n].append(ps)
 
         def finish(n):
             b, j = n // J, n % J
-            ots = []
+            terms = 2 if n in PE_ADD else 1
+            dst = out[b, 2 * j : 2 * j + 2].rearrange("h (p a) d -> p h a d", a=A)
+            blocks = A // len(prod[n])
             for half in range(2):
-                ots.append(psum.tile([P, 2, 2, P], F32, name="ot", tag="ot"))
-            for par in range(2):
-                for a in range(A):
-                    nc.tensor.transpose(ots[a // 2][:, a % 2, par, :], prod[n][par][:, P * a : P * (a + 1)], ident_f[:])
-            res = work.tile([P, 2, A, D], F32, name="res", tag="res", bufs=3)
-            for a in range(A):
-                nc.scalar.activation(
-                    out=res[:, :, a, :].rearrange("p h (i r) -> p h i r", r=2),
-                    in_=ots[a // 2][:, a % 2].rearrange("p r (h i) -> p h i r", h=2),
-                    func=RELU,
-                )
-            nc.sync.dma_start(
-                out=out[b, 2 * j : 2 * j + 2].rearrange("h (p a) d -> p h (a d)", a=A),
-                in_=res[:].rearrange("p h a d -> p h (a d)"),
-            )
+                ot = psum.tile([P, 2, 2, P], F32, name="ot", tag="ot")
+                for par in range(2):
+                    for al in range(2):
+                        a = 2 * half + al
+                        for e in range(terms):
+                            nc.tensor.matmul(
+                                out=ot[:, par, al, :],
+                                lhsT=prod[n][a // blocks][e][:, par, P * (a % blocks) : P * (a % blocks + 1)],
+                                rhs=ident_f[:],
+                                is_transpose=True,
+                                start=(e == 0),
+                                stop=(e == terms - 1),
+                            )
+                res = work.tile([P, 2, 2, D], F32, name="res", tag="res", bufs=4)
+                res_view = res[:].rearrange("p h a (i r) -> p a h i r", r=2)
+                ot_view = ot[:].rearrange("p r a (h i) -> p a h i r", h=2)
+                if n == UNITS - 1 and half == 1:
+                    nc.vector.tensor_scalar_max(out=res_view, in0=ot_view, scalar1=0.0)
+                else:
+                    nc.scalar.activation(out=res_view, in_=ot_view, func=RELU)
+                nc.sync.dma_start(out=dst[:, :, 2 * half : 2 * half + 2, :], in_=res[:])
 
+        new_codes(0)
         for c in range(A):
             x_transpose(c)
-        tabs = []
-        for t in range(4):
-            tp = psum.tile([P, S], BF16, name="tp", tag="ot")
-            for a in range(A):
-                nc.tensor.transpose(tp[:, P * a : P * (a + 1)], stg[:, t, a, :], ident_b[:])
-            tab = const.tile([P, S], BF16, name="tab%d" % t, tag="tab%d" % t)
-            nc.scalar.copy(out=tab[:], in_=tp[:])
-            tabs.append(tab)
-        quantize(0)
-        for c in range(A, LEAD):
-            x_transpose(c)
+            quantize_chunk(c)
+        dummy_matmuls(WARM[2])
 
+        chunk = A
         for n in range(UNITS + LAG):
-            if n + LEAD < UNITS:
-                x_transpose(n + LEAD)
+            if n < UNITS:
+                matmuls(n)
+            while chunk < B * A and chunk <= n + LEAD:
+                x_transpose(chunk)
+                chunk += 1
             if n >= LAG:
                 finish(n - LAG)
             if n < UNITS:
-                matmuls(n)
                 if n % J == J - 1 and n + 1 < UNITS:
                     quantize(n // J + 1)
                 rope(n)

@@ -25,7 +25,9 @@ J = 4
 UNITS = B * J
 LAG = 3
 LEAD = 5
-PE_ADD = (2, 6, 10, 14, 15)
+PE_ADD = (14, 15)
+OUT_BANKS = {13: ("xt", "xt"), 14: ("acc0", "acc1")}
+VECTOR_RELU = ((14, 1), (15, 1))
 WARM = (6, 2, 2)
 
 
@@ -156,14 +158,16 @@ def tile_lineartransformerblock_pa_kernel(tc, x, cos, sin, Wq_words, Wq_scales, 
                     in_=grouped[0][:, a, g].rearrange("p c u -> p (c u)").bitcast(BF16),
                 )
 
+        fence = const.tile([P, 8], U32, name="fence", tag="fence")
+
         def quantize(b):
             new_codes(b)
-            for g in range(G):
-                nc.vector.quantize_mx(
-                    out=xq[b][:, g, :].bitcast(E5X4),
-                    scales=xs[b][:, g, :],
-                    in_=grouped[b][:, g].rearrange("p c u -> p (c u)").bitcast(BF16),
-                )
+            nc.vector.quantize_mx(
+                out=xq[b][:].rearrange("p g c -> p (g c)").bitcast(E5X4),
+                scales=xs[b][:].rearrange("p g c -> p (g c)"),
+                in_=grouped[b][:].rearrange("p g c u -> p (g c u)").bitcast(BF16),
+            )
+            nc.gpsimd.tensor_copy(out=fence[:], in_=xq[b][:, G - 1, S - 8 : S])
 
         acc = {}
         prod = {}
@@ -204,6 +208,8 @@ def tile_lineartransformerblock_pa_kernel(tc, x, cos, sin, Wq_words, Wq_scales, 
                         op0=ADD,
                         op1=MULT,
                     )
+                if n % J == J - 2 and n + 2 < UNITS:
+                    quantize(n // J + 1)
                 if n not in PE_ADD:
                     nc.gpsimd.tensor_tensor(out=ps[0][:], in0=ps[0][:], in1=ps[1][:], op=ADD)
                 prod[n].append(ps)
@@ -214,7 +220,7 @@ def tile_lineartransformerblock_pa_kernel(tc, x, cos, sin, Wq_words, Wq_scales, 
             dst = out[b, 2 * j : 2 * j + 2].rearrange("h (p a) d -> p h a d", a=A)
             blocks = A // len(prod[n])
             for half in range(2):
-                ot = psum.tile([P, 2, 2, P], F32, name="ot", tag="ot")
+                ot = psum.tile([P, 2, 2, P], F32, name="ot", tag=OUT_BANKS.get(n, ("ot", "ot"))[half])
                 for par in range(2):
                     for al in range(2):
                         a = 2 * half + al
@@ -227,10 +233,10 @@ def tile_lineartransformerblock_pa_kernel(tc, x, cos, sin, Wq_words, Wq_scales, 
                                 start=(e == 0),
                                 stop=(e == terms - 1),
                             )
-                res = work.tile([P, 2, 2, D], F32, name="res", tag="res", bufs=4)
+                res = work.tile([P, 2, 2, D], F32, name="res", tag="res", bufs=6)
                 res_view = res[:].rearrange("p h a (i r) -> p a h i r", r=2)
                 ot_view = ot[:].rearrange("p r a (h i) -> p a h i r", h=2)
-                if n == UNITS - 1 and half == 1:
+                if (n, half) in VECTOR_RELU:
                     nc.vector.tensor_scalar_max(out=res_view, in0=ot_view, scalar1=0.0)
                 else:
                     nc.scalar.activation(out=res_view, in_=ot_view, func=RELU)
@@ -252,6 +258,4 @@ def tile_lineartransformerblock_pa_kernel(tc, x, cos, sin, Wq_words, Wq_scales, 
             if n >= LAG:
                 finish(n - LAG)
             if n < UNITS:
-                if n % J == J - 1 and n + 1 < UNITS:
-                    quantize(n // J + 1)
                 rope(n)

@@ -28,7 +28,7 @@ LEAD = 5
 PE_ADD = (14, 15)
 OUT_BANKS = {13: ("xt", "xt"), 14: ("acc0", "acc1")}
 VECTOR_RELU = ((14, 1), (15, 1))
-WARM = (6, 2, 2)
+WARM = (4, 0, 2)
 
 
 def tile_lineartransformerblock_pa_kernel(tc, x, cos, sin, Wq_words, Wq_scales, bq, out):
@@ -44,11 +44,6 @@ def tile_lineartransformerblock_pa_kernel(tc, x, cos, sin, Wq_words, Wq_scales, 
 
         ws_raw = const.tile([P, G, H * D], U8, name="ws_raw", tag="ws_raw", align_bytes=64)
         nc.gpsimd.memset(ws_raw[:].rearrange("p g n -> p (g n)").bitcast(F32), 0.0)
-        for q4 in range(4):
-            nc.sync.dma_start(
-                out=ws_raw[32 * q4 : 32 * q4 + 4, :, :].bitcast(I32),
-                in_=Wq_scales[:, 4 * q4 : 4 * q4 + 4, :].rearrange("g r n -> r g n").bitcast(I32),
-            )
 
         cos_raw = const.tile([P, A, D], BF16, name="cos_raw", tag="cos_raw")
         sin_raw = const.tile([P, A, D], BF16, name="sin_raw", tag="sin_raw")
@@ -58,6 +53,11 @@ def tile_lineartransformerblock_pa_kernel(tc, x, cos, sin, Wq_words, Wq_scales, 
         w_raw = const.tile([P, G, 2 * H * D], U8, name="w_raw", tag="w_raw", align_bytes=64)
         for g in range(G):
             nc.sync.dma_start(out=w_raw[:, g, :].bitcast(I32), in_=Wq_words[g].bitcast(I32))
+        for q4 in range(4):
+            nc.sync.dma_start(
+                out=ws_raw[32 * q4 : 32 * q4 + 4, :, :].bitcast(I32),
+                in_=Wq_scales[:, 4 * q4 : 4 * q4 + 4, :].rearrange("g r n -> r g n").bitcast(I32),
+            )
 
         x_sb = []
         for b in range(B):
@@ -113,19 +113,17 @@ def tile_lineartransformerblock_pa_kernel(tc, x, cos, sin, Wq_words, Wq_scales, 
         wp = const.tile([P, G, J, 2, 2 * P], U8, name="wp", tag="wp", align_bytes=64)
         wsp = const.tile([P, G, J, 2, P], U8, name="wsp", tag="wsp", align_bytes=64)
         for g in range(G):
-            for par in range(2):
-                nc.vector.tensor_copy(
-                    out=wp[:, g, :, par, :].rearrange("p j (q t) -> p j q t", t=2),
-                    in_=w_raw[:, g, :].rearrange("p (j q r t) -> p j q r t", j=J, r=2, t=2)[:, :, :, par, :],
-                )
+            nc.vector.tensor_copy(
+                out=wp[:, g].rearrange("p j r (q t) -> p j r q t", t=2),
+                in_=w_raw[:, g, :].rearrange("p (j q r t) -> p j r q t", j=J, r=2, t=2),
+            )
         for g in range(G):
-            for par in range(2):
-                nc.vector.tensor_copy(
-                    out=wsp[:, g, :, par, :],
-                    in_=ws_raw[:, g, :].rearrange("p (j q r) -> p j q r", j=J, r=2)[:, :, :, par],
-                )
+            nc.vector.tensor_copy(
+                out=wsp[:, g],
+                in_=ws_raw[:, g, :].rearrange("p (j q r) -> p j r q", j=J, r=2),
+            )
         bias = const.tile([P, J, 2], F32, name="bias", tag="bias")
-        nc.vector.tensor_copy(out=bias[:], in_=bias_bf[:])
+        nc.gpsimd.tensor_copy(out=bias[:], in_=bias_bf[:])
 
         grouped = {}
         xq = {}

@@ -17,6 +17,7 @@ ADD = mybir.AluOpType.add
 MULT = mybir.AluOpType.mult
 RELU = mybir.ActivationFunctionType.Relu
 COPY = mybir.ActivationFunctionType.Copy
+IDENT = mybir.ActivationFunctionType.Identity
 
 P = 128
 G = 2
@@ -25,7 +26,8 @@ J = 4
 UNITS = B * J
 LAG = 3
 LEAD = 5
-PE_ADD = (14, 15)
+PE_ADD = (0, 14, 15)
+G_MUL = ((0, 0), (15, 1))
 OUT_BANKS = {13: ("xt", "xt"), 14: ("acc0", "acc1")}
 VECTOR_RELU = ((14, 1), (15, 1))
 WARM = (4, 0, 2)
@@ -188,9 +190,24 @@ def tile_lineartransformerblock_pa_kernel(tc, x, cos, sin, Wq_words, Wq_scales, 
                 tiles.append(t)
             acc[n] = tiles
 
+        biased = {}
+
+        def pieces_of(n):
+            return 2 if n == UNITS - 1 else 1
+
+        def add_bias_on_scalar(n):
+            width = S // pieces_of(n)
+            for piece in range(pieces_of(n)):
+                if (n, piece) in G_MUL:
+                    cols = slice(piece * width, (piece + 1) * width)
+                    biased[n] = work.tile([P, S], F32, name="biased", tag="biased")
+                    nc.scalar.activation(
+                        out=biased[n][:, cols], in_=acc[n][1][:, cols], func=IDENT, bias=bias[:, n % J, 1:2]
+                    )
+
         def rope(n):
             j = n % J
-            pieces = 2 if n == UNITS - 1 else 1
+            pieces = pieces_of(n)
             width = S // pieces
             prod[n] = []
             for piece in range(pieces):
@@ -198,6 +215,14 @@ def tile_lineartransformerblock_pa_kernel(tc, x, cos, sin, Wq_words, Wq_scales, 
                 ps = []
                 for e in range(2):
                     ps.append(work.tile([P, 2, width], F32, name="prod%d" % e, tag="prod%d" % e, bufs=LAG + 1))
+                    if e == 1 and (n, piece) in G_MUL:
+                        nc.gpsimd.tensor_tensor(
+                            out=ps[e][:],
+                            in0=biased[n][:, cols].unsqueeze(1).to_broadcast([P, 2, width]),
+                            in1=tabs[e][:, :, cols],
+                            op=MULT,
+                        )
+                        continue
                     nc.vector.scalar_tensor_tensor(
                         out=ps[e][:],
                         in0=acc[n][e][:, cols].unsqueeze(1).to_broadcast([P, 2, width]),
@@ -250,6 +275,7 @@ def tile_lineartransformerblock_pa_kernel(tc, x, cos, sin, Wq_words, Wq_scales, 
         for n in range(UNITS + LAG):
             if n < UNITS:
                 matmuls(n)
+                add_bias_on_scalar(n)
             while chunk < B * A and chunk <= n + LEAD:
                 x_transpose(chunk)
                 chunk += 1

@@ -26,7 +26,7 @@ J = 4
 UNITS = B * J
 LAG = 3
 LEAD = 5
-PE_ADD = (0, 14, 15)
+PE_ADD = (0, 3, 6, 9, 12, 14, 15)
 G_MUL = ((0, 0), (15, 1))
 OUT_BANKS = {13: ("xt", "xt"), 14: ("acc0", "acc1")}
 VECTOR_RELU = ((14, 1), (15, 1))

@@ -47,27 +47,42 @@ def tile_lineartransformerblock_pa_kernel(tc, x, cos, sin, Wq_words, Wq_scales, 
         ws_raw = const.tile([P, G, H * D], U8, name="ws_raw", tag="ws_raw", align_bytes=64)
         nc.gpsimd.memset(ws_raw[:].rearrange("p g n -> p (g n)").bitcast(F32), 0.0)
 
-        cos_raw = const.tile([P, A, D], BF16, name="cos_raw", tag="cos_raw")
-        sin_raw = const.tile([P, A, D], BF16, name="sin_raw", tag="sin_raw")
-        nc.sync.dma_start(out=cos_raw[:], in_=cos.rearrange("(p a) d -> p a d", a=A))
-        nc.sync.dma_start(out=sin_raw[:], in_=sin.rearrange("(p a) d -> p a d", a=A))
-
-        w_raw = const.tile([P, G, 2 * H * D], U8, name="w_raw", tag="w_raw", align_bytes=64)
-        for g in range(G):
-            nc.sync.dma_start(out=w_raw[:, g, :].bitcast(I32), in_=Wq_words[g].bitcast(I32))
-        for q4 in range(4):
-            nc.sync.dma_start(
-                out=ws_raw[32 * q4 : 32 * q4 + 4, :, :].bitcast(I32),
-                in_=Wq_scales[:, 4 * q4 : 4 * q4 + 4, :].rearrange("g r n -> r g n").bitcast(I32),
-            )
-
         x_sb = []
         for b in range(B):
             x_sb.append(const.tile([P, A, C], BF16, name="x_sb%d" % b, tag="x_sb%d" % b))
         x_view = x.rearrange("b (p a) k -> b p a k", a=A)
         for a in range(A):
             nc.sync.dma_start(out=x_sb[0][:, a, :], in_=x_view[0, :, a, :])
-        for b in range(1, B):
+
+        words_view = Wq_words.rearrange("g p n -> p g n")
+        w_raw = []
+        for j in range(J):
+            w_raw.append(const.tile([P, G, 4 * P], U8, name="w_raw%d" % j, tag="w_raw%d" % j, align_bytes=64))
+
+        def load_words(j):
+            nc.sync.dma_start(
+                out=w_raw[j][:].bitcast(I32), in_=words_view[:, :, 4 * P * j : 4 * P * (j + 1)].bitcast(I32)
+            )
+
+        load_words(0)
+        for q4 in range(4):
+            nc.sync.dma_start(
+                out=ws_raw[32 * q4 : 32 * q4 + 4, :, :].bitcast(I32),
+                in_=Wq_scales[:, 4 * q4 : 4 * q4 + 4, :].rearrange("g r n -> r g n").bitcast(I32),
+            )
+        trig_raw = const.tile([P, 2, A, 2, D], BF16, name="trig_raw", tag="trig_raw")
+        for tb, src in enumerate((cos, sin)):
+            nc.sync.dma_start(
+                out=trig_raw[:, tb],
+                in_=src.rearrange("(p a) d -> p a d", a=A).unsqueeze(2).to_broadcast([P, A, 2, D]),
+            )
+        load_words(1)
+        for a in range(A):
+            nc.sync.dma_start(out=x_sb[1][:, a, :], in_=x_view[1, :, a, :])
+            if a == 1:
+                load_words(2)
+                load_words(3)
+        for b in range(2, B):
             nc.sync.dma_start(out=x_sb[b][:], in_=x_view[b])
 
         zeros = const.tile([P, S], BF16, name="zeros", tag="zeros")
@@ -77,8 +92,6 @@ def tile_lineartransformerblock_pa_kernel(tc, x, cos, sin, Wq_words, Wq_scales, 
         nc.vector.memset(warm_in[:], 0.0)
         nc.scalar.activation(out=warm_out[:], in_=warm_in[:], func=RELU)
 
-        ident_b = const.tile([P, P], BF16, name="ident_b", tag="ident_b")
-        make_identity(nc, ident_b[:])
         ident_f = const.tile([P, P], F32, name="ident_f", tag="ident_f")
         make_identity(nc, ident_f[:])
 
@@ -89,43 +102,43 @@ def tile_lineartransformerblock_pa_kernel(tc, x, cos, sin, Wq_words, Wq_scales, 
 
         dummy_matmuls(WARM[0])
 
-        stg = const.tile([P, 2, 2, A, P], BF16, name="stg", tag="stg")
-
-        def spread(src, par):
-            return src[:, :, par::2].unsqueeze(2).to_broadcast([P, A, 2, D // 2])
-
-        def stg_view(e, t):
-            return stg[:, e, t].rearrange("p a (h i) -> p a h i", h=2)
-
-        nc.vector.tensor_copy(out=stg_view(0, 0), in_=spread(cos_raw, 0))
-        nc.vector.tensor_copy(out=stg_view(1, 1), in_=spread(cos_raw, 1))
-        nc.scalar.activation(out=stg_view(0, 1), in_=spread(sin_raw, 1), func=COPY)
-        nc.scalar.activation(out=stg_view(1, 0), in_=spread(sin_raw, 0), func=COPY, scale=-1.0)
-
         tabs = []
         for e in range(2):
             tabs.append(const.tile([P, 2, S], BF16, name="tab%d" % e, tag="tab%d" % e))
-        for e, t, bank in ((0, 0, "ot"), (1, 1, "ot"), (0, 1, "acc1"), (1, 0, "acc1")):
-            tp = psum.tile([P, S], BF16, name="tp", tag=bank)
-            for a in range(A):
-                nc.tensor.transpose(tp[:, P * a : P * (a + 1)], stg[:, e, t, a, :], ident_b[:])
-            nc.scalar.copy(out=tabs[e][:, t, :], in_=tp[:])
-        dummy_matmuls(WARM[1])
 
-        wp = const.tile([P, G, J, 2, 2 * P], U8, name="wp", tag="wp", align_bytes=64)
-        wsp = const.tile([P, G, J, 2, P], U8, name="wsp", tag="wsp", align_bytes=64)
-        for g in range(G):
-            nc.vector.tensor_copy(
-                out=wp[:, g].rearrange("p j r (q t) -> p j r q t", t=2),
-                in_=w_raw[:, g, :].rearrange("p (j q r t) -> p j r q t", j=J, r=2, t=2),
-            )
-        for g in range(G):
-            nc.vector.tensor_copy(
-                out=wsp[:, g],
-                in_=ws_raw[:, g, :].rearrange("p (j q r) -> p j r q", j=J, r=2),
-            )
+        def make_tables():
+            halves = []
+            for tb in range(2):
+                tp = psum.tile([P, S], F32, name="tp", tag="ot")
+                for a in range(A):
+                    nc.tensor.transpose(
+                        tp[:, P * a : P * (a + 1)],
+                        trig_raw[:, tb, a].rearrange("p h d -> p (h d)").bitcast(F32),
+                        ident_f[:],
+                    )
+                halves.append(tp[:].bitcast(BF16).rearrange("p (s r) -> p r s", r=2))
+            nc.vector.tensor_copy(out=tabs[0][:, 0, :], in_=halves[0][:, 0, :])
+            nc.vector.tensor_copy(out=tabs[1][:, 1, :], in_=halves[0][:, 1, :])
+            nc.scalar.copy(out=tabs[0][:, 1, :], in_=halves[1][:, 1, :])
+            nc.scalar.activation(out=tabs[1][:, 0, :], in_=halves[1][:, 0, :], func=COPY, scale=-1.0)
+
         bias = const.tile([P, J, 2], F32, name="bias", tag="bias")
         nc.gpsimd.tensor_copy(out=bias[:], in_=bias_bf[:])
+        wp = []
+        wsp = []
+        for j in range(J):
+            wp.append(const.tile([P, G, 2, 2 * P], U8, name="wp%d" % j, tag="wp%d" % j, align_bytes=64))
+            wsp.append(const.tile([P, G, 2, P], U8, name="wsp%d" % j, tag="wsp%d" % j, align_bytes=64))
+
+        def sort_weights(j):
+            nc.vector.tensor_copy(
+                out=wp[j][:].rearrange("p g r (q t) -> p g r q t", t=2),
+                in_=w_raw[j][:].rearrange("p g (q r t) -> p g r q t", r=2, t=2),
+            )
+            nc.vector.tensor_copy(
+                out=wsp[j][:],
+                in_=ws_raw[:, :, 2 * P * j : 2 * P * (j + 1)].rearrange("p g (q r) -> p g r q", r=2),
+            )
 
         grouped = {}
         xq = {}
@@ -180,8 +193,8 @@ def tile_lineartransformerblock_pa_kernel(tc, x, cos, sin, Wq_words, Wq_scales, 
                 for g in range(G):
                     nc.tensor.matmul_mx(
                         out=t[:],
-                        lhsT=wp[:, g, j, par, :].bitcast(E2X4),
-                        lhsT_scale=wsp[:, g, j, par, :],
+                        lhsT=wp[j][:, g, par, :].bitcast(E2X4),
+                        lhsT_scale=wsp[j][:, g, par, :],
                         rhs=xq[b][:, g, :].bitcast(E5X4),
                         rhs_scale=xs[b][:, g, :],
                         start=(g == 0),
@@ -269,6 +282,10 @@ def tile_lineartransformerblock_pa_kernel(tc, x, cos, sin, Wq_words, Wq_scales, 
         for c in range(A):
             x_transpose(c)
             quantize_chunk(c)
+            if c == 1:
+                sort_weights(0)
+        make_tables()
+        sort_weights(1)
         dummy_matmuls(WARM[2])
 
         chunk = A
@@ -283,3 +300,5 @@ def tile_lineartransformerblock_pa_kernel(tc, x, cos, sin, Wq_words, Wq_scales, 
                 finish(n - LAG)
             if n < UNITS:
                 rope(n)
+            if n + 2 < J:
+                sort_weights(n + 2)

@@ -144,6 +144,16 @@ def tile_lineartransformerblock_pa_kernel(tc, x, cos, sin, Wq_words, Wq_scales, 
         xq = {}
         xs = {}
 
+        sorted_words = {}
+
+        def x_sort(c):
+            b, a = c // A, c % A
+            sorted_words[c] = work.tile([P, G, 2, P], F32, name="xw", tag="xw", bufs=4)
+            nc.scalar.copy(
+                out=sorted_words[c][:],
+                in_=x_sb[b][:, a, :].bitcast(F32).rearrange("p (g q u) -> p g u q", g=G, u=2),
+            )
+
         def x_transpose(c):
             b, a = c // A, c % A
             if a == 0:
@@ -155,7 +165,10 @@ def tile_lineartransformerblock_pa_kernel(tc, x, cos, sin, Wq_words, Wq_scales, 
             xt = psum.tile([P, G, 2, P], F32, name="xt", tag="xt")
             for g in range(G):
                 for u in range(2):
-                    nc.tensor.transpose(xt[:, g, u, :], words[:, 256 * g + u : 256 * (g + 1) : 2], ident_f[:])
+                    if c in sorted_words:
+                        nc.tensor.transpose(xt[:, g, u, :], sorted_words[c][:, g, u, :], ident_f[:])
+                    else:
+                        nc.tensor.transpose(xt[:, g, u, :], words[:, 256 * g + u : 256 * (g + 1) : 2], ident_f[:])
             dst = grouped[b][:, a] if b == 0 else grouped[b][:, :, P * a : P * (a + 1), :]
             nc.scalar.copy(out=dst, in_=xt[:].rearrange("p g u r -> p g r u"))
 
@@ -293,6 +306,8 @@ def tile_lineartransformerblock_pa_kernel(tc, x, cos, sin, Wq_words, Wq_scales, 
             if n < UNITS:
                 matmuls(n)
                 add_bias_on_scalar(n)
+            if n + LEAD + 2 < B * A:
+                x_sort(n + LEAD + 2)
             while chunk < B * A and chunk <= n + LEAD:
                 x_transpose(chunk)
                 chunk += 1

@@ -26,11 +26,11 @@ J = 4
 UNITS = B * J
 LAG = 3
 LEAD = 5
-PE_ADD = (0, 3, 6, 9, 12, 14, 15)
+PE_ADD = (0, 3, 5, 9, 12, 14, 15)
 G_MUL = ((0, 0), (15, 1))
 OUT_BANKS = {13: ("xt", "xt"), 14: ("acc0", "acc1")}
 VECTOR_RELU = ((14, 1), (15, 1))
-WARM = (4, 0, 2)
+WARM = (4, 0, 0)
 
 
 def tile_lineartransformerblock_pa_kernel(tc, x, cos, sin, Wq_words, Wq_scales, bq, out):

@@ -26,7 +26,7 @@ J = 4
 UNITS = B * J
 LAG = 3
 LEAD = 5
-PE_ADD = (0, 3, 5, 9, 12, 14, 15)
+PE_ADD = (0, 1, 5, 9, 12, 14, 15)
 G_MUL = ((0, 0), (15, 1))
 OUT_BANKS = {13: ("xt", "xt"), 14: ("acc0", "acc1")}
 VECTOR_RELU = ((14, 1), (15, 1))

@@ -27,7 +27,7 @@ UNITS = B * J
 LAG = 3
 LEAD = 5
 PE_ADD = (0, 1, 5, 9, 12, 14, 15)
-G_MUL = ((0, 0), (15, 1))
+G_MUL = ((0, 0), (1, 0), (15, 1))
 OUT_BANKS = {13: ("xt", "xt"), 14: ("acc0", "acc1")}
 VECTOR_RELU = ((14, 1), (15, 1))
 WARM = (4, 0, 0)
@@ -117,9 +117,9 @@ def tile_lineartransformerblock_pa_kernel(tc, x, cos, sin, Wq_words, Wq_scales, 
                         ident_f[:],
                     )
                 halves.append(tp[:].bitcast(BF16).rearrange("p (s r) -> p r s", r=2))
-            nc.vector.tensor_copy(out=tabs[0][:, 0, :], in_=halves[0][:, 0, :])
-            nc.vector.tensor_copy(out=tabs[1][:, 1, :], in_=halves[0][:, 1, :])
+            nc.scalar.copy(out=tabs[0][:, 0, :], in_=halves[0][:, 0, :])
             nc.scalar.copy(out=tabs[0][:, 1, :], in_=halves[1][:, 1, :])
+            nc.scalar.copy(out=tabs[1][:, 1, :], in_=halves[0][:, 1, :])
             nc.scalar.activation(out=tabs[1][:, 0, :], in_=halves[1][:, 0, :], func=COPY, scale=-1.0)
 
         bias = const.tile([P, J, 2], F32, name="bias", tag="bias")
@@ -306,7 +306,7 @@ def tile_lineartransformerblock_pa_kernel(tc, x, cos, sin, Wq_words, Wq_scales, 
             if n < UNITS:
                 matmuls(n)
                 add_bias_on_scalar(n)
-            if n + LEAD + 2 < B * A:
+            if 0 < n and n + LEAD + 2 < B * A:
                 x_sort(n + LEAD + 2)
             while chunk < B * A and chunk <= n + LEAD:
                 x_transpose(chunk)

@@ -41,11 +41,19 @@ def tile_lineartransformerblock_pa_kernel(tc, x, cos, sin, Wq_words, Wq_scales, 
         psum = ctx.enter_context(tc.psum_pool(name="psum", bufs=2))
         ctx.enter_context(tc.manual_schedule())
 
-        bias_bf = const.tile([P, J, 2], BF16, name="bias_bf", tag="bias_bf")
-        nc.scalar.dma_start(out=bias_bf[:], in_=bq.rearrange("(j q r) -> q j r", j=J, r=2))
-
         ws_raw = const.tile([P, G, H * D], U8, name="ws_raw", tag="ws_raw", align_bytes=64)
         nc.gpsimd.memset(ws_raw[:].rearrange("p g n -> p (g n)").bitcast(F32), 0.0)
+
+        words_view = Wq_words.rearrange("g p n -> p g n")
+        w_first = const.tile([P, G, 4 * P], U8, name="w_first", tag="w_first", align_bytes=64)
+        w_rest = const.tile([P, G, 4 * P * (J - 1)], U8, name="w_rest", tag="w_rest", align_bytes=64)
+        nc.sync.dma_start(out=w_first[:].bitcast(I32), in_=words_view[:, :, 0 : 4 * P].bitcast(I32))
+        nc.sync.dma_start(out=w_rest[:].bitcast(I32), in_=words_view[:, :, 4 * P : 4 * P * J].bitcast(I32))
+        for q4 in range(4):
+            nc.sync.dma_start(
+                out=ws_raw[32 * q4 : 32 * q4 + 4, :, :].bitcast(I32),
+                in_=Wq_scales[:, 4 * q4 : 4 * q4 + 4, :].rearrange("g r n -> r g n").bitcast(I32),
+            )
 
         x_sb = []
         for b in range(B):
@@ -54,34 +62,16 @@ def tile_lineartransformerblock_pa_kernel(tc, x, cos, sin, Wq_words, Wq_scales, 
         for a in range(A):
             nc.sync.dma_start(out=x_sb[0][:, a, :], in_=x_view[0, :, a, :])
 
-        words_view = Wq_words.rearrange("g p n -> p g n")
-        w_raw = []
-        for j in range(J):
-            w_raw.append(const.tile([P, G, 4 * P], U8, name="w_raw%d" % j, tag="w_raw%d" % j, align_bytes=64))
-
-        def load_words(j):
-            nc.sync.dma_start(
-                out=w_raw[j][:].bitcast(I32), in_=words_view[:, :, 4 * P * j : 4 * P * (j + 1)].bitcast(I32)
-            )
-
-        load_words(0)
-        for q4 in range(4):
-            nc.sync.dma_start(
-                out=ws_raw[32 * q4 : 32 * q4 + 4, :, :].bitcast(I32),
-                in_=Wq_scales[:, 4 * q4 : 4 * q4 + 4, :].rearrange("g r n -> r g n").bitcast(I32),
-            )
         trig_raw = const.tile([P, 2, A, 2, D], BF16, name="trig_raw", tag="trig_raw")
         for tb, src in enumerate((cos, sin)):
             nc.sync.dma_start(
                 out=trig_raw[:, tb],
                 in_=src.rearrange("(p a) d -> p a d", a=A).unsqueeze(2).to_broadcast([P, A, 2, D]),
             )
-        load_words(1)
+        bias_bf = const.tile([P, J, 2], BF16, name="bias_bf", tag="bias_bf")
+        nc.sync.dma_start(out=bias_bf[:], in_=bq.rearrange("(j q r) -> q j r", j=J, r=2))
         for a in range(A):
             nc.sync.dma_start(out=x_sb[1][:, a, :], in_=x_view[1, :, a, :])
-            if a == 1:
-                load_words(2)
-                load_words(3)
         for b in range(2, B):
             nc.sync.dma_start(out=x_sb[b][:], in_=x_view[b])
 
@@ -133,7 +123,9 @@ def tile_lineartransformerblock_pa_kernel(tc, x, cos, sin, Wq_words, Wq_scales, 
         def sort_weights(j):
             nc.vector.tensor_copy(
                 out=wp[j][:].rearrange("p g r (q t) -> p g r q t", t=2),
-                in_=w_raw[j][:].rearrange("p g (q r t) -> p g r q t", r=2, t=2),
+                in_=(w_first[:] if j == 0 else w_rest[:, :, 4 * P * (j - 1) : 4 * P * j]).rearrange(
+                    "p g (q r t) -> p g r q t", r=2, t=2
+                ),
             )
             nc.vector.tensor_copy(
                 out=wsp[j][:],
@@ -292,13 +284,12 @@ def tile_lineartransformerblock_pa_kernel(tc, x, cos, sin, Wq_words, Wq_scales, 
                 nc.sync.dma_start(out=dst[:, :, 2 * half : 2 * half + 2, :], in_=res[:])
 
         new_codes(0)
+        for j in range(J):
+            sort_weights(j)
         for c in range(A):
             x_transpose(c)
             quantize_chunk(c)
-            if c == 1:
-                sort_weights(0)
         make_tables()
-        sort_weights(1)
         dummy_matmuls(WARM[2])
 
         chunk = A
@@ -315,5 +306,3 @@ def tile_lineartransformerblock_pa_kernel(tc, x, cos, sin, Wq_words, Wq_scales, 
                 finish(n - LAG)
             if n < UNITS:
                 rope(n)
-            if n + 2 < J:
-                sort_weights(n + 2)

@@ -27,7 +27,7 @@ UNITS = B * J
 LAG = 3
 LEAD = 5
 PE_ADD = (0, 1, 5, 9, 12, 14, 15)
-G_MUL = ((0, 0), (1, 0), (15, 1))
+G_MUL = ((0, 0), (15, 1))
 OUT_BANKS = {13: ("xt", "xt"), 14: ("acc0", "acc1")}
 VECTOR_RELU = ((14, 1), (15, 1))
 WARM = (4, 0, 0)

@@ -294,12 +294,13 @@ def tile_lineartransformerblock_pa_kernel(tc, x, cos, sin, Wq_words, Wq_scales, 
 
         chunk = A
         for n in range(UNITS + LAG):
-            if n < UNITS:
-                matmuls(n)
-                add_bias_on_scalar(n)
+            for m in ((0, 1) if n == 0 else () if n == 1 else (n,)):
+                if m < UNITS:
+                    matmuls(m)
+                    add_bias_on_scalar(m)
             if 0 < n and n + LEAD + 2 < B * A:
                 x_sort(n + LEAD + 2)
-            while chunk < B * A and chunk <= n + LEAD:
+            while chunk < B * A and chunk <= n + LEAD and n != 1:
                 x_transpose(chunk)
                 chunk += 1
             if n >= LAG:

@@ -107,13 +107,13 @@ def tile_lineartransformerblock_pa_kernel(tc, x, cos, sin, Wq_words, Wq_scales, 
                         ident_f[:],
                     )
                 halves.append(tp[:].bitcast(BF16).rearrange("p (s r) -> p r s", r=2))
+            nc.scalar.copy(out=bias[:], in_=bias_bf[:])
             nc.scalar.copy(out=tabs[0][:, 0, :], in_=halves[0][:, 0, :])
             nc.scalar.copy(out=tabs[0][:, 1, :], in_=halves[1][:, 1, :])
             nc.scalar.copy(out=tabs[1][:, 1, :], in_=halves[0][:, 1, :])
             nc.scalar.activation(out=tabs[1][:, 0, :], in_=halves[1][:, 0, :], func=COPY, scale=-1.0)
 
         bias = const.tile([P, J, 2], F32, name="bias", tag="bias")
-        nc.gpsimd.tensor_copy(out=bias[:], in_=bias_bf[:])
         wp = []
         wsp = []
         for j in range(J):
@@ -121,13 +121,14 @@ def tile_lineartransformerblock_pa_kernel(tc, x, cos, sin, Wq_words, Wq_scales, 
             wsp.append(const.tile([P, G, 2, P], U8, name="wsp%d" % j, tag="wsp%d" % j, align_bytes=64))
 
         def sort_weights(j):
-            nc.vector.tensor_copy(
+            mover = nc.gpsimd if j == J - 1 else nc.vector
+            mover.tensor_copy(
                 out=wp[j][:].rearrange("p g r (q t) -> p g r q t", t=2),
                 in_=(w_first[:] if j == 0 else w_rest[:, :, 4 * P * (j - 1) : 4 * P * j]).rearrange(
                     "p g (q r t) -> p g r q t", r=2, t=2
                 ),
             )
-            nc.vector.tensor_copy(
+            mover.tensor_copy(
                 out=wsp[j][:],
                 in_=ws_raw[:, :, 2 * P * j : 2 * P * (j + 1)].rearrange("p g (q r) -> p g r q", r=2),
             )

from contextlib import ExitStack

import concourse.mybir as mybir
from concourse.masks import make_identity

B, S, C, H, D = 4, 512, 1024, 8, 128
FLOPS = 2 * B * S * C * H * D

F32 = mybir.dt.float32
BF16 = mybir.dt.bfloat16
U32 = mybir.dt.uint32
U8 = mybir.dt.uint8
I32 = mybir.dt.int32
E5X4 = mybir.dt.float8_e5m2_x4
E2X4 = mybir.dt.float4_e2m1fn_x4
ADD = mybir.AluOpType.add
MULT = mybir.AluOpType.mult
RELU = mybir.ActivationFunctionType.Relu
COPY = mybir.ActivationFunctionType.Copy
IDENT = mybir.ActivationFunctionType.Identity

P = 128
G = 2
A = 4
J = 4
UNITS = B * J
LAG = 3
LEAD = 5
PE_ADD = (0, 1, 5, 9, 12, 14, 15)
G_MUL = ((0, 0), (15, 1))
OUT_BANKS = {13: ("xt", "xt"), 14: ("acc0", "acc1")}
VECTOR_RELU = ((14, 1), (15, 1))
WARM = (4, 0, 0)


def tile_lineartransformerblock_pa_kernel(tc, x, cos, sin, Wq_words, Wq_scales, bq, out):
    nc = tc.nc
    with ExitStack() as ctx:
        const = ctx.enter_context(tc.tile_pool(name="const", bufs=1))
        work = ctx.enter_context(tc.tile_pool(name="work", bufs=2))
        psum = ctx.enter_context(tc.psum_pool(name="psum", bufs=2))
        ctx.enter_context(tc.manual_schedule())

        ws_raw = const.tile([P, G, H * D], U8, name="ws_raw", tag="ws_raw", align_bytes=64)
        nc.gpsimd.memset(ws_raw[:].rearrange("p g n -> p (g n)").bitcast(F32), 0.0)

        words_view = Wq_words.rearrange("g p n -> p g n")
        w_first = const.tile([P, G, 4 * P], U8, name="w_first", tag="w_first", align_bytes=64)
        w_rest = const.tile([P, G, 4 * P * (J - 1)], U8, name="w_rest", tag="w_rest", align_bytes=64)
        nc.sync.dma_start(out=w_first[:].bitcast(I32), in_=words_view[:, :, 0 : 4 * P].bitcast(I32))
        nc.sync.dma_start(out=w_rest[:].bitcast(I32), in_=words_view[:, :, 4 * P : 4 * P * J].bitcast(I32))
        for q4 in range(4):
            nc.sync.dma_start(
                out=ws_raw[32 * q4 : 32 * q4 + 4, :, :].bitcast(I32),
                in_=Wq_scales[:, 4 * q4 : 4 * q4 + 4, :].rearrange("g r n -> r g n").bitcast(I32),
            )

        x_sb = []
        for b in range(B):
            x_sb.append(const.tile([P, A, C], BF16, name="x_sb%d" % b, tag="x_sb%d" % b))
        x_view = x.rearrange("b (p a) k -> b p a k", a=A)
        for a in range(A):
            nc.sync.dma_start(out=x_sb[0][:, a, :], in_=x_view[0, :, a, :])

        trig_raw = const.tile([P, 2, A, 2, D], BF16, name="trig_raw", tag="trig_raw")
        for tb, src in enumerate((cos, sin)):
            nc.sync.dma_start(
                out=trig_raw[:, tb],
                in_=src.rearrange("(p a) d -> p a d", a=A).unsqueeze(2).to_broadcast([P, A, 2, D]),
            )
        bias_bf = const.tile([P, J, 2], BF16, name="bias_bf", tag="bias_bf")
        nc.sync.dma_start(out=bias_bf[:], in_=bq.rearrange("(j q r) -> q j r", j=J, r=2))
        for a in range(A):
            nc.sync.dma_start(out=x_sb[1][:, a, :], in_=x_view[1, :, a, :])
        for b in range(2, B):
            nc.sync.dma_start(out=x_sb[b][:], in_=x_view[b])

        zeros = const.tile([P, S], BF16, name="zeros", tag="zeros")
        nc.vector.memset(zeros[:], 0.0)
        warm_in = const.tile([P, 1], F32, name="warm_in", tag="warm_in")
        warm_out = const.tile([P, 1], F32, name="warm_out", tag="warm_out")
        nc.vector.memset(warm_in[:], 0.0)
        nc.scalar.activation(out=warm_out[:], in_=warm_in[:], func=RELU)

        ident_f = const.tile([P, P], F32, name="ident_f", tag="ident_f")
        make_identity(nc, ident_f[:])

        def dummy_matmuls(count):
            for w in range(count):
                d_ps = psum.tile([P, S], F32, name="d_ps", tag="acc0")
                nc.tensor.matmul(out=d_ps[:], lhsT=zeros[:, 0:P], rhs=zeros[:], start=True, stop=True)

        dummy_matmuls(WARM[0])

        tabs = []
        for e in range(2):
            tabs.append(const.tile([P, 2, S], BF16, name="tab%d" % e, tag="tab%d" % e))

        def make_tables():
            halves = []
            for tb in range(2):
                tp = psum.tile([P, S], F32, name="tp", tag="ot")
                for a in range(A):
                    nc.tensor.transpose(
                        tp[:, P * a : P * (a + 1)],
                        trig_raw[:, tb, a].rearrange("p h d -> p (h d)").bitcast(F32),
                        ident_f[:],
                    )
                halves.append(tp[:].bitcast(BF16).rearrange("p (s r) -> p r s", r=2))
            nc.scalar.copy(out=bias[:], in_=bias_bf[:])
            nc.scalar.copy(out=tabs[0][:, 0, :], in_=halves[0][:, 0, :])
            nc.scalar.copy(out=tabs[0][:, 1, :], in_=halves[1][:, 1, :])
            nc.scalar.copy(out=tabs[1][:, 1, :], in_=halves[0][:, 1, :])
            nc.scalar.activation(out=tabs[1][:, 0, :], in_=halves[1][:, 0, :], func=COPY, scale=-1.0)

        bias = const.tile([P, J, 2], F32, name="bias", tag="bias")
        wp = []
        wsp = []
        for j in range(J):
            wp.append(const.tile([P, G, 2, 2 * P], U8, name="wp%d" % j, tag="wp%d" % j, align_bytes=64))
            wsp.append(const.tile([P, G, 2, P], U8, name="wsp%d" % j, tag="wsp%d" % j, align_bytes=64))

        def sort_weights(j):
            mover = nc.gpsimd if j == J - 1 else nc.vector
            mover.tensor_copy(
                out=wp[j][:].rearrange("p g r (q t) -> p g r q t", t=2),
                in_=(w_first[:] if j == 0 else w_rest[:, :, 4 * P * (j - 1) : 4 * P * j]).rearrange(
                    "p g (q r t) -> p g r q t", r=2, t=2
                ),
            )
            mover.tensor_copy(
                out=wsp[j][:],
                in_=ws_raw[:, :, 2 * P * j : 2 * P * (j + 1)].rearrange("p g (q r) -> p g r q", r=2),
            )

        grouped = {}
        xq = {}
        xs = {}

        sorted_words = {}

        def x_sort(c):
            b, a = c // A, c % A
            sorted_words[c] = work.tile([P, G, 2, P], F32, name="xw", tag="xw", bufs=4)
            nc.scalar.copy(
                out=sorted_words[c][:],
                in_=x_sb[b][:, a, :].bitcast(F32).rearrange("p (g q u) -> p g u q", g=G, u=2),
            )

        def x_transpose(c):
            b, a = c // A, c % A
            if a == 0:
                if b == 0:
                    grouped[b] = const.tile([P, A, G, P, 2], F32, name="grouped0", tag="grouped0", align_bytes=64)
                else:
                    grouped[b] = work.tile([P, G, S, 2], F32, name="grouped", tag="grouped", align_bytes=64)
            words = x_sb[b][:, a, :].bitcast(F32)
            xt = psum.tile([P, G, 2, P], F32, name="xt", tag="xt")
            for g in range(G):
                for u in range(2):
                    if c in sorted_words:
                        nc.tensor.transpose(xt[:, g, u, :], sorted_words[c][:, g, u, :], ident_f[:])
                    else:
                        nc.tensor.transpose(xt[:, g, u, :], words[:, 256 * g + u : 256 * (g + 1) : 2], ident_f[:])
            dst = grouped[b][:, a] if b == 0 else grouped[b][:, :, P * a : P * (a + 1), :]
            nc.scalar.copy(out=dst, in_=xt[:].rearrange("p g u r -> p g r u"))

        def new_codes(b):
            xq[b] = work.tile([P, G, S], U32, name="xq", tag="xq", align_bytes=64)
            xs[b] = work.tile([P, G, S], U8, name="xs", tag="xs", align_bytes=64)

        def quantize_chunk(a):
            for g in range(G):
                nc.vector.quantize_mx(
                    out=xq[0][:, g, P * a : P * (a + 1)].bitcast(E5X4),
                    scales=xs[0][:, g, P * a : P * (a + 1)],
                    in_=grouped[0][:, a, g].rearrange("p c u -> p (c u)").bitcast(BF16),
                )

        fence = const.tile([P, 8], U32, name="fence", tag="fence")

        def quantize(b):
            new_codes(b)
            nc.vector.quantize_mx(
                out=xq[b][:].rearrange("p g c -> p (g c)").bitcast(E5X4),
                scales=xs[b][:].rearrange("p g c -> p (g c)"),
                in_=grouped[b][:].rearrange("p g c u -> p (g c u)").bitcast(BF16),
            )
            nc.gpsimd.tensor_copy(out=fence[:], in_=xq[b][:, G - 1, S - 8 : S])

        acc = {}
        prod = {}

        def matmuls(n):
            b, j = n // J, n % J
            tiles = []
            for par in range(2):
                t = psum.tile([P, S], F32, name="acc%d" % par, tag="acc%d" % par)
                for g in range(G):
                    nc.tensor.matmul_mx(
                        out=t[:],
                        lhsT=wp[j][:, g, par, :].bitcast(E2X4),
                        lhsT_scale=wsp[j][:, g, par, :],
                        rhs=xq[b][:, g, :].bitcast(E5X4),
                        rhs_scale=xs[b][:, g, :],
                        start=(g == 0),
                        stop=(g == G - 1),
                    )
                tiles.append(t)
            acc[n] = tiles

        biased = {}

        def pieces_of(n):
            return 2 if n == UNITS - 1 else 1

        def add_bias_on_scalar(n):
            width = S // pieces_of(n)
            for piece in range(pieces_of(n)):
                if (n, piece) in G_MUL:
                    cols = slice(piece * width, (piece + 1) * width)
                    biased[n] = work.tile([P, S], F32, name="biased", tag="biased")
                    nc.scalar.activation(
                        out=biased[n][:, cols], in_=acc[n][1][:, cols], func=IDENT, bias=bias[:, n % J, 1:2]
                    )

        def rope(n):
            j = n % J
            pieces = pieces_of(n)
            width = S // pieces
            prod[n] = []
            for piece in range(pieces):
                cols = slice(piece * width, (piece + 1) * width)
                ps = []
                for e in range(2):
                    ps.append(work.tile([P, 2, width], F32, name="prod%d" % e, tag="prod%d" % e, bufs=LAG + 1))
                    if e == 1 and (n, piece) in G_MUL:
                        nc.gpsimd.tensor_tensor(
                            out=ps[e][:],
                            in0=biased[n][:, cols].unsqueeze(1).to_broadcast([P, 2, width]),
                            in1=tabs[e][:, :, cols],
                            op=MULT,
                        )
                        continue
                    nc.vector.scalar_tensor_tensor(
                        out=ps[e][:],
                        in0=acc[n][e][:, cols].unsqueeze(1).to_broadcast([P, 2, width]),
                        scalar=bias[:, j, e : e + 1],
                        in1=tabs[e][:, :, cols],
                        op0=ADD,
                        op1=MULT,
                    )
                if n % J == J - 2 and n + 2 < UNITS:
                    quantize(n // J + 1)
                if n not in PE_ADD:
                    nc.gpsimd.tensor_tensor(out=ps[0][:], in0=ps[0][:], in1=ps[1][:], op=ADD)
                prod[n].append(ps)

        def finish(n):
            b, j = n // J, n % J
            terms = 2 if n in PE_ADD else 1
            dst = out[b, 2 * j : 2 * j + 2].rearrange("h (p a) d -> p h a d", a=A)
            blocks = A // len(prod[n])
            for half in range(2):
                ot = psum.tile([P, 2, 2, P], F32, name="ot", tag=OUT_BANKS.get(n, ("ot", "ot"))[half])
                for par in range(2):
                    for al in range(2):
                        a = 2 * half + al
                        for e in range(terms):
                            nc.tensor.matmul(
                                out=ot[:, par, al, :],
                                lhsT=prod[n][a // blocks][e][:, par, P * (a % blocks) : P * (a % blocks + 1)],
                                rhs=ident_f[:],
                                is_transpose=True,
                                start=(e == 0),
                                stop=(e == terms - 1),
                            )
                res = work.tile([P, 2, 2, D], F32, name="res", tag="res", bufs=6)
                res_view = res[:].rearrange("p h a (i r) -> p a h i r", r=2)
                ot_view = ot[:].rearrange("p r a (h i) -> p a h i r", h=2)
                if (n, half) in VECTOR_RELU:
                    nc.vector.tensor_scalar_max(out=res_view, in0=ot_view, scalar1=0.0)
                else:
                    nc.scalar.activation(out=res_view, in_=ot_view, func=RELU)
                nc.sync.dma_start(out=dst[:, :, 2 * half : 2 * half + 2, :], in_=res[:])

        new_codes(0)
        for j in range(J):
            sort_weights(j)
        for c in range(A):
            x_transpose(c)
            quantize_chunk(c)
        make_tables()
        dummy_matmuls(WARM[2])

        chunk = A
        for n in range(UNITS + LAG):
            for m in ((0, 1) if n == 0 else () if n == 1 else (n,)):
                if m < UNITS:
                    matmuls(m)
                    add_bias_on_scalar(m)
            if 0 < n and n + LEAD + 2 < B * A:
                x_sort(n + LEAD + 2)
            while chunk < B * A and chunk <= n + LEAD and n != 1:
                x_transpose(chunk)
                chunk += 1
            if n >= LAG:
                finish(n - LAG)
            if n < UNITS:
                rope(n)
